import numpy as np
import ml_dtypes

BF16 = ml_dtypes.bfloat16


def bf(x):
    return np.asarray(x, np.float32).astype(BF16)


def f32(x):
    return np.asarray(x, np.float32)


def f64(x):
    return np.asarray(x).astype(np.float64)


def striped(idx):
    return np.tile(idx.reshape(-1, 16).T, (8, 1))


C, S, N, Q, U = 256, 2048, 768, 2, 384


def setup_inputs():
    return {
        "base": f32(np.random.standard_normal((C, S))),
        "x_self": f32(np.random.standard_normal((C, N))),
        "x_nb": bf(np.random.standard_normal((N, C))),
        "adj_t": bf(2.0 * np.random.uniform(size=(N, U)) / np.sqrt(U)),
        "offs": striped(np.random.permutation(S)[:N]),
    }


def reference(base, x_self, x_nb, adj_t, offs):
    idx = offs[:16].T.reshape(-1)
    xs, xn, at = f64(x_self), f64(x_nb), f64(adj_t)
    res = f64(base).copy()
    for q in range(Q):
        r = slice(q * U, (q + 1) * U)
        res[:, idx[r]] = xs[:, r] + xn[r].T @ at[r]
    return res

@@ -1,0 +1,55 @@
+import concourse.mybir as mybir
+
+F32, BF16, U16 = mybir.dt.float32, mybir.dt.bfloat16, mybir.dt.uint16
+
+P = 128
+C, S, N, Q, U = 256, 2048, 768, 2, 384
+CHANNEL_BLOCKS = C // P
+SENDER_BLOCKS = U // P
+
+FLOPS = 2 * C * N * U
+
+
+def tile_gnn_kernel(tc, base, x_self, x_nb, adj_t, offs, out):
+    nc = tc.nc
+    add = mybir.AluOpType.add
+    copy = mybir.ActivationFunctionType.Copy
+
+    with (
+        tc.tile_pool(name="held", bufs=1) as held,
+        tc.psum_pool(name="psum", bufs=1) as psum,
+    ):
+        offsets = held.tile([P, N // 16], U16, name="offsets")
+        nc.sync.dma_start(offsets[:], offs)
+
+        senders = held.tile([P, Q, SENDER_BLOCKS, C], BF16, name="senders")
+        nc.scalar.dma_start(senders[:], x_nb.rearrange("(q p k) c -> p q k c", q=Q, p=P))
+        edges = held.tile([P, Q, SENDER_BLOCKS, U], BF16, name="edges")
+        nc.sync.dma_start(edges[:], adj_t.rearrange("(q p k) i -> p q k i", q=Q, p=P))
+
+        own = []
+        windows = []
+        for cb in range(CHANNEL_BLOCKS):
+            rows = slice(cb * P, (cb + 1) * P)
+            own.append(held.tile([P, N], F32, name=f"own{cb}"))
+            nc.scalar.dma_start(own[cb][:], x_self[rows, :])
+            windows.append(held.tile([P, S], F32, name=f"window{cb}"))
+            nc.sync.dma_start(windows[cb][:], base[rows, :])
+
+        for cb in range(CHANNEL_BLOCKS):
+            rows = slice(cb * P, (cb + 1) * P)
+            messages = held.tile([P, N], F32, name=f"messages{cb}")
+            for q in range(Q):
+                summed = psum.tile([P, U], F32, name=f"summed{cb}{q}")
+                for k in range(SENDER_BLOCKS):
+                    nc.tensor.matmul(
+                        summed[:],
+                        senders[:, q, k, rows],
+                        edges[:, q, k, :],
+                        start=(k == 0),
+                        stop=(k == SENDER_BLOCKS - 1),
+                    )
+                nc.scalar.activation(messages[:, q * U : (q + 1) * U], summed[:], copy)
+
+            nc.vector.tensor_tensor(windows[cb][:].indirect(offsets[:]), messages[:], own[cb][:], add)
+            nc.sync.dma_start(out[rows, :], windows[cb][:])

@@ -23,16 +23,19 @@ def tile_gnn_kernel(tc, base, x_self, x_nb, adj_t, offs, out):
         nc.sync.dma_start(offsets[:], offs)
 
         senders = held.tile([P, Q, SENDER_BLOCKS, C], BF16, name="senders")
-        nc.scalar.dma_start(senders[:], x_nb.rearrange("(q p k) c -> p q k c", q=Q, p=P))
         edges = held.tile([P, Q, SENDER_BLOCKS, U], BF16, name="edges")
-        nc.sync.dma_start(edges[:], adj_t.rearrange("(q p k) i -> p q k i", q=Q, p=P))
+        senders_dram = x_nb.rearrange("(q p k) c -> p q k c", q=Q, p=P)
+        edges_dram = adj_t.rearrange("(q p k) i -> p q k i", q=Q, p=P)
+        for q in range(Q):
+            nc.sync.dma_start(senders[:, q], senders_dram[:, q])
+            nc.sync.dma_start(edges[:, q], edges_dram[:, q])
 
         own = []
         windows = []
         for cb in range(CHANNEL_BLOCKS):
             rows = slice(cb * P, (cb + 1) * P)
             own.append(held.tile([P, N], F32, name=f"own{cb}"))
-            nc.scalar.dma_start(own[cb][:], x_self[rows, :])
+            nc.sync.dma_start(own[cb][:], x_self[rows, :])
             windows.append(held.tile([P, S], F32, name=f"window{cb}"))
             nc.sync.dma_start(windows[cb][:], base[rows, :])
 

@@ -55,4 +55,5 @@ def tile_gnn_kernel(tc, base, x_self, x_nb, adj_t, offs, out):
                 nc.scalar.activation(messages[:, q * U : (q + 1) * U], summed[:], copy)
 
             nc.vector.tensor_tensor(windows[cb][:].indirect(offsets[:]), messages[:], own[cb][:], add)
-            nc.sync.dma_start(out[rows, :], windows[cb][:])
+            nc.sync.dma_start(out[rows, 0 : S // 2], windows[cb][:, 0 : S // 2])
+            nc.scalar.dma_start(out[rows, S // 2 : S], windows[cb][:, S // 2 : S])

@@ -6,6 +6,7 @@ P = 128
 C, S, N, Q, U = 256, 2048, 768, 2, 384
 CHANNEL_BLOCKS = C // P
 SENDER_BLOCKS = U // P
+ALIGN = 256
 
 FLOPS = 2 * C * N * U
 
@@ -22,8 +23,8 @@ def tile_gnn_kernel(tc, base, x_self, x_nb, adj_t, offs, out):
         offsets = held.tile([P, N // 16], U16, name="offsets")
         nc.sync.dma_start(offsets[:], offs)
 
-        senders = held.tile([P, Q, SENDER_BLOCKS, C], BF16, name="senders")
-        edges = held.tile([P, Q, SENDER_BLOCKS, U], BF16, name="edges")
+        senders = held.tile([P, Q, SENDER_BLOCKS, C], BF16, name="senders", align_bytes=ALIGN)
+        edges = held.tile([P, Q, SENDER_BLOCKS, U], BF16, name="edges", align_bytes=ALIGN)
         senders_dram = x_nb.rearrange("(q p k) c -> p q k c", q=Q, p=P)
         edges_dram = adj_t.rearrange("(q p k) i -> p q k i", q=Q, p=P)
         for q in range(Q):
@@ -34,9 +35,9 @@ def tile_gnn_kernel(tc, base, x_self, x_nb, adj_t, offs, out):
         windows = []
         for cb in range(CHANNEL_BLOCKS):
             rows = slice(cb * P, (cb + 1) * P)
-            own.append(held.tile([P, N], F32, name=f"own{cb}"))
+            own.append(held.tile([P, N], F32, name=f"own{cb}", align_bytes=ALIGN))
             nc.sync.dma_start(own[cb][:], x_self[rows, :])
-            windows.append(held.tile([P, S], F32, name=f"window{cb}"))
+            windows.append(held.tile([P, S], F32, name=f"window{cb}", align_bytes=ALIGN))
             nc.sync.dma_start(windows[cb][:], base[rows, :])
 
         for cb in range(CHANNEL_BLOCKS):

@@ -6,7 +6,7 @@ P = 128
 C, S, N, Q, U = 256, 2048, 768, 2, 384
 CHANNEL_BLOCKS = C // P
 SENDER_BLOCKS = U // P
-ALIGN = 256
+ALIGN = 4096
 
 FLOPS = 2 * C * N * U
 

import concourse.mybir as mybir

F32, BF16, U16 = mybir.dt.float32, mybir.dt.bfloat16, mybir.dt.uint16

P = 128
C, S, N, Q, U = 256, 2048, 768, 2, 384
CHANNEL_BLOCKS = C // P
SENDER_BLOCKS = U // P
ALIGN = 4096

FLOPS = 2 * C * N * U


def tile_gnn_kernel(tc, base, x_self, x_nb, adj_t, offs, out):
    nc = tc.nc
    add = mybir.AluOpType.add
    copy = mybir.ActivationFunctionType.Copy

    with (
        tc.tile_pool(name="held", bufs=1) as held,
        tc.psum_pool(name="psum", bufs=1) as psum,
    ):
        offsets = held.tile([P, N // 16], U16, name="offsets")
        nc.sync.dma_start(offsets[:], offs)

        senders = held.tile([P, Q, SENDER_BLOCKS, C], BF16, name="senders", align_bytes=ALIGN)
        edges = held.tile([P, Q, SENDER_BLOCKS, U], BF16, name="edges", align_bytes=ALIGN)
        senders_dram = x_nb.rearrange("(q p k) c -> p q k c", q=Q, p=P)
        edges_dram = adj_t.rearrange("(q p k) i -> p q k i", q=Q, p=P)
        for q in range(Q):
            nc.sync.dma_start(senders[:, q], senders_dram[:, q])
            nc.sync.dma_start(edges[:, q], edges_dram[:, q])

        own = []
        windows = []
        for cb in range(CHANNEL_BLOCKS):
            rows = slice(cb * P, (cb + 1) * P)
            own.append(held.tile([P, N], F32, name=f"own{cb}", align_bytes=ALIGN))
            nc.sync.dma_start(own[cb][:], x_self[rows, :])
            windows.append(held.tile([P, S], F32, name=f"window{cb}", align_bytes=ALIGN))
            nc.sync.dma_start(windows[cb][:], base[rows, :])

        for cb in range(CHANNEL_BLOCKS):
            rows = slice(cb * P, (cb + 1) * P)
            messages = held.tile([P, N], F32, name=f"messages{cb}")
            for q in range(Q):
                summed = psum.tile([P, U], F32, name=f"summed{cb}{q}")
                for k in range(SENDER_BLOCKS):
                    nc.tensor.matmul(
                        summed[:],
                        senders[:, q, k, rows],
                        edges[:, q, k, :],
                        start=(k == 0),
                        stop=(k == SENDER_BLOCKS - 1),
                    )
                nc.scalar.activation(messages[:, q * U : (q + 1) * U], summed[:], copy)

            nc.vector.tensor_tensor(windows[cb][:].indirect(offsets[:]), messages[:], own[cb][:], add)
            nc.sync.dma_start(out[rows, 0 : S // 2], windows[cb][:, 0 : S // 2])
            nc.scalar.dma_start(out[rows, S // 2 : S], windows[cb][:, S // 2 : S])
